import numpy as np
import ml_dtypes


def mxq(x, axis, fmt="e4m3"):
    dtype, down = {"e4m3": (ml_dtypes.float8_e4m3fn, 7), "e5m2": (ml_dtypes.float8_e5m2, 14)}[fmt]
    v = np.moveaxis(np.asarray(x, np.float32).astype(ml_dtypes.bfloat16).astype(np.float64), axis, -1)
    blocks = v.reshape(v.shape[:-1] + (-1, 32))
    amax = np.abs(blocks).max(-1, keepdims=True)
    byte = np.maximum(np.where(amax > 0, np.frexp(amax)[1] - 1 + 127, 0) - down, 1)
    scale = np.exp2(byte - 127.0)
    codes = (blocks / scale).astype(np.float32).astype(dtype).astype(np.float64)
    return np.moveaxis((codes * scale).reshape(v.shape), -1, axis)


WIDE = False


def mx_kscale(k):
    if not WIDE:
        return np.ones(k)
    levels = np.array([10, -10, 5, -5, 0])
    a = np.random.permutation(np.resize(levels, k // 512 * 4)).reshape(k // 512, 4)
    idx = np.arange(k)
    return np.exp2(a[idx // 512, idx % 128 // 32])


BF16 = ml_dtypes.bfloat16


def bf(x):
    return np.asarray(x, np.float32).astype(BF16)


def f64(x):
    return np.asarray(x).astype(np.float64)


B, L, D = 2, 1024, 512


def setup_inputs():
    t = mx_kscale(L)
    t = t / t.min()
    u = 1.0 / t.max()
    c, h, q = D // 32, D // 2, D // 4
    tr = t[None, :, None]
    sh = np.log(tr) * np.sqrt(D) / c
    x1 = np.random.standard_normal((B, L, D)) * 1.25
    x2 = np.random.standard_normal((B, L, D)) * 1.25
    x1[:, :, :c] = x1[:, :, :c] * u + (1.0 - u)
    x2[:, :, :c] -= sh
    x1[:, :, h:h + q] *= u
    x2[:, :, h:h + q] *= tr
    x2[:, :, c:2 * c] = x2[:, :, c:2 * c] * u + (1.0 - u)
    x1[:, :, c:2 * c] -= sh
    x2[:, :, h + q:] *= u
    x1[:, :, h + q:] *= tr
    return {"x1": bf(x1), "x2": bf(x2)}


def reference(x1, x2):
    x1, x2 = f64(x1), f64(x2)
    scale = 1.0 / np.sqrt(D)
    s = (x1 @ x2.transpose(0, 2, 1)) * scale
    ea = np.exp(s - s.max(-1, keepdims=True))
    out_a = (mxq(ea, 2, "e4m3") @ mxq(x2, 1, "e4m3")) / ea.sum(-1, keepdims=True)
    st = s.transpose(0, 2, 1)
    eb = np.exp(st - st.max(-1, keepdims=True))
    out_b = (mxq(eb, 2, "e4m3") @ mxq(x1, 1, "e4m3")) / eb.sum(-1, keepdims=True)
    return out_a + out_b

@@ -1,0 +1,258 @@
+from contextlib import ExitStack
+import math
+
+import concourse.mybir as mybir
+from concourse.masks import make_identity
+
+F32 = mybir.dt.float32
+BF16 = mybir.dt.bfloat16
+U32 = mybir.dt.uint32
+U8 = mybir.dt.uint8
+FP8X4 = mybir.dt.float8_e4m3fn_x4
+ALU = mybir.AluOpType
+ACT = mybir.ActivationFunctionType
+
+P = 128
+B, L, D = 2, 1024, 512
+TILES = L // P
+SCALE = 1.0 / math.sqrt(D)
+FLOPS = 3 * 2 * B * L * L * D
+
+LAG_EXP = 1
+LAG_TR = 2
+LAG_Q = 3
+LAG_MX = 4
+
+
+def tile_mutualcrossattention_kernel(tc, x1, x2, out):
+    nc = tc.nc
+    dram = {"x1": x1, "x2": x2}
+    with ExitStack() as ctx:
+        const = ctx.enter_context(tc.tile_pool(name="const", bufs=1))
+        xin = ctx.enter_context(tc.tile_pool(name="xin", bufs=1))
+        xtp = ctx.enter_context(tc.tile_pool(name="xtp", bufs=1))
+        xqp = ctx.enter_context(tc.tile_pool(name="xqp", bufs=1))
+        xgp = ctx.enter_context(tc.tile_pool(name="xgp", bufs=2))
+        ssb = ctx.enter_context(tc.tile_pool(name="ssb", bufs=1))
+        stp = ctx.enter_context(tc.tile_pool(name="stp", bufs=3))
+        ep = ctx.enter_context(tc.tile_pool(name="ep", bufs=4))
+        gp = ctx.enter_context(tc.tile_pool(name="gp", bufs=3))
+        tmpp = ctx.enter_context(tc.tile_pool(name="tmpp", bufs=10))
+        otp = ctx.enter_context(tc.tile_pool(name="otp", bufs=3))
+        small = ctx.enter_context(tc.tile_pool(name="small", bufs=8))
+        psum = ctx.enter_context(tc.psum_pool(name="psum", bufs=2))
+
+        ident_f = const.tile([P, P], F32, name="ident_f", tag="ident_f")
+        ident_b = const.tile([P, P], BF16, name="ident_b", tag="ident_b")
+
+        keys = [(x, b) for b in range(B) for x in ("x2", "x1")]
+        raw, xt, xcodes, xscales = {}, {}, {}, {}
+        for x, b in keys:
+            nm = "%s_%d" % (x, b)
+            raw[x, b] = xin.tile([P, TILES, D], BF16, name="raw_" + nm, tag="raw_" + nm)
+            xt[x, b] = xtp.tile([P, 2, 2 * L], BF16, name="xt_" + nm, tag="xt_" + nm)
+            xcodes[x, b] = xqp.tile([P, 2, D], U32, name="xc_" + nm, tag="xc_" + nm, align_bytes=64)
+            xscales[x, b] = xqp.tile([P, 2, D], U8, name="xs_" + nm, tag="xs_" + nm, align_bytes=64)
+
+        def load(x, b, c):
+            src = dram[x][b].rearrange("(c q e) d -> q c (e d)", c=4, q=P, e=2)
+            dst = raw[x, b][:].rearrange("q (c e) d -> q c (e d)", e=2)
+            nc.sync.dma_start(out=dst[:, c, :], in_=src[:, c, :])
+
+        for b in range(B):
+            for half in range(2):
+                for x in ("x2", "x1"):
+                    for c in (2 * half, 2 * half + 1):
+                        load(x, b, c)
+
+        make_identity(nc, ident_f[:])
+        make_identity(nc, ident_b[:])
+
+        copy_turn = [0]
+
+        def transpose_x(x, b, w, h, tag, engine=None):
+            words = raw[x, b][:].bitcast(F32)
+            bank = psum.tile([P, 4, P], F32, name="xbank", tag=tag, bufs=(4 if tag == "r" else 2))
+            for k in range(4):
+                nc.tensor.transpose(bank[:, k, :], words[:, 4 * h + k, P * w:P * (w + 1)], ident_f[:])
+            dst = xt[x, b][:].bitcast(F32)[:, w, 512 * h:512 * (h + 1)]
+            src = bank[:].rearrange("p k q -> p (k q)")
+            if engine is None:
+                engine = ("v", "s")[copy_turn[0] % 2]
+                copy_turn[0] += 1
+            if engine == "v":
+                nc.vector.tensor_copy(out=dst, in_=src)
+            else:
+                nc.scalar.copy(out=dst, in_=src)
+
+        grouped = {}
+
+        def regroup_x(x, b, g):
+            t = xgp.tile([P, D, 4], BF16, name="xg", tag="xg", align_bytes=64)
+            grouped[x, b, g] = t
+            nc.vector.tensor_copy(
+                out=t[:].rearrange("p (c i) t -> p c t i", i=4),
+                in_=raw[x, b][:, 4 * g:4 * g + 4, :].rearrange("p t (c i) -> p c t i", i=4),
+            )
+
+        def quantise_x(x, b, g):
+            nc.vector.quantize_mx(
+                out=xcodes[x, b][:, g, :].bitcast(FP8X4),
+                scales=xscales[x, b][:, g, :],
+                in_=grouped[x, b, g][:].rearrange("p d t -> p (d t)"),
+            )
+
+        blocks = [("s", 0, k) for k in range(TILES)]
+        for k in range(TILES):
+            blocks += [("s", 1, k), ("t", 0, k)]
+        blocks += [("t", 1, k) for k in range(TILES)]
+        n_blocks = len(blocks)
+
+        saved = {}
+        st = [dict() for blk in blocks]
+        tmp = {}
+
+        def fill_half(n, h):
+            kind, b, k = blocks[n]
+            bank = psum.tile([P, 4, P], F32, name="rbank", tag="r", bufs=4)
+            st[n]["bank%d" % h] = bank
+            if kind == "s":
+                a = xt["x1", b][:].rearrange("p w (n e) -> p w n e", e=2)
+                m = xt["x2", b][:].rearrange("p w (n e) -> p w n e", e=2)
+                flat = bank[:].rearrange("p k q -> p (k q)")
+                for c in range(4):
+                    w, e = c // 2, c % 2
+                    nc.tensor.matmul(
+                        out=flat,
+                        lhsT=a[:, w, P * k:P * (k + 1), e],
+                        rhs=m[:, w, 512 * h:512 * (h + 1), e],
+                        start=(c == 0),
+                        stop=(c == 3),
+                    )
+            else:
+                for j in range(4):
+                    nc.tensor.transpose(bank[:, j, :], saved[b, 4 * h + j][:, P * k:P * (k + 1)], ident_f[:])
+
+        def evacuate_half(n, h):
+            kind, b, k = blocks[n]
+            if h == 0:
+                if kind == "s":
+                    rows = ssb.tile([P, L], F32, name="s_%d_%d" % (b, k), tag="s_%d_%d" % (b, k))
+                    saved[b, k] = rows
+                else:
+                    rows = stp.tile([P, L], F32, name="st", tag="st")
+                st[n]["rows"] = rows
+                st[n]["nb0"] = small.tile([P, 1], F32, name="nb0", tag="nb0")
+                st[n]["nb"] = small.tile([P, 1], F32, name="nb", tag="nb")
+            nc.vector.tensor_scalar(
+                out=st[n]["rows"][:, 512 * h:512 * (h + 1)],
+                in0=st[n]["bank%d" % h][:].rearrange("p k q -> p (k q)"),
+                scalar1=(-SCALE if kind == "s" else 1.0),
+                scalar2=(None if h == 0 else st[n]["nb0"][:, 0:1]),
+                op0=ALU.mult,
+                op1=ALU.min,
+                accum_out=(st[n]["nb0"] if h == 0 else st[n]["nb"])[:, 0:1],
+            )
+
+        def exponentials(n):
+            e = ep.tile([P, L], BF16, name="e", tag="e")
+            st[n]["e"] = e
+            st[n]["sum"] = small.tile([P, 1], F32, name="sum", tag="sum")
+            nc.scalar.activation(
+                out=e[:], in_=st[n]["rows"][:], func=ACT.Exp, bias=st[n]["nb"][:, 0:1], scale=-1.0,
+                accum_out=st[n]["sum"][:, 0:1],
+            )
+
+        def transpose_e(n):
+            et = psum.tile([P, TILES, P], BF16, name="et", tag="t", bufs=2)
+            st[n]["et"] = et
+            for c in range(TILES):
+                nc.tensor.transpose(et[:, c, :], st[n]["e"][:, P * c:P * (c + 1)], ident_b[:])
+
+        def regroup_e(n):
+            g = gp.tile([P, 2, P, 4], BF16, name="g", tag="g", align_bytes=64)
+            st[n]["g"] = g
+            nc.scalar.copy(out=g[:], in_=st[n]["et"][:].rearrange("p (g t) r -> p g r t", g=2))
+
+        def quantise_e(n):
+            st[n]["codes"] = gp.tile([P, 2 * P], U32, name="codes", tag="codes", align_bytes=64)
+            st[n]["scales"] = gp.tile([P, 2 * P], U8, name="scales", tag="scales", align_bytes=64)
+            nc.vector.quantize_mx(
+                out=st[n]["codes"][:].bitcast(FP8X4),
+                scales=st[n]["scales"][:],
+                in_=st[n]["g"][:].rearrange("p g r t -> p (g r t)"),
+            )
+            st[n]["rec"] = small.tile([P, 1], F32, name="rec", tag="rec")
+            nc.vector.reciprocal(out=st[n]["rec"][:, 0:1], in_=st[n]["sum"][:, 0:1])
+
+        def product(n):
+            kind, b, k = blocks[n]
+            x = "x2" if kind == "s" else "x1"
+            acc = psum.tile([P, D], F32, name="acc", tag="o", bufs=2)
+            st[n]["acc"] = acc
+            for g in range(2):
+                nc.tensor.matmul_mx(
+                    out=acc[:],
+                    lhsT=st[n]["codes"][:, P * g:P * (g + 1)].bitcast(FP8X4),
+                    lhsT_scale=st[n]["scales"][:, P * g:P * (g + 1)],
+                    rhs=xcodes[x, b][:, g, :].bitcast(FP8X4),
+                    rhs_scale=xscales[x, b][:, g, :],
+                    start=(g == 0),
+                    stop=(g == 1),
+                )
+
+        def finish(n):
+            kind, b, k = blocks[n]
+            if kind == "s":
+                t = tmpp.tile([P, D], F32, name="tmp", tag="tmp")
+                tmp[b, k] = t
+                if n < TILES:
+                    nc.scalar.activation(out=t[:], in_=st[n]["acc"][:], func=ACT.Copy, scale=st[n]["rec"][:, 0:1])
+                else:
+                    nc.vector.tensor_scalar(
+                        out=t[:], in0=st[n]["acc"][:], scalar1=st[n]["rec"][:, 0:1], scalar2=None, op0=ALU.mult
+                    )
+            else:
+                o = otp.tile([P, D], F32, name="o", tag="o")
+                nc.vector.scalar_tensor_tensor(
+                    out=o[:], in0=st[n]["acc"][:], scalar=st[n]["rec"][:, 0:1], in1=tmp[b, k][:],
+                    op0=ALU.mult, op1=ALU.add,
+                )
+                dst = out[b].rearrange("(c q e) d -> c e q d", c=4, q=P, e=2)
+                nc.sync.dma_start(out=dst[k // 2, k % 2], in_=o[:])
+
+        for x, w, h in (("x2", 0, 0), ("x2", 1, 0), ("x1", 0, 0), ("x1", 1, 0), ("x2", 0, 1), ("x2", 1, 1)):
+            transpose_x(x, 0, w, h, "r")
+
+        tensor_extras = {
+            1: [("x1", 0, 0, 1), ("x1", 0, 1, 1)],
+            2: [("x2", 1, 0, 0), ("x2", 1, 1, 0)],
+            3: [("x2", 1, 0, 1), ("x2", 1, 1, 1)],
+            4: [("x1", 1, 0, 0), ("x1", 1, 1, 0)],
+            5: [("x1", 1, 0, 1), ("x1", 1, 1, 1)],
+        }
+        units = []
+        for x, b in (("x2", 0), ("x1", 0), ("x2", 1), ("x1", 1)):
+            units += [[(regroup_x, x, b, 0)], [(regroup_x, x, b, 1)], [(quantise_x, x, b, 0), (quantise_x, x, b, 1)]]
+
+        for n in range(n_blocks + LAG_MX + 1):
+            if 0 <= n - LAG_Q < n_blocks:
+                quantise_e(n - LAG_Q)
+            if n < len(units):
+                for fn, x, b, g in units[n]:
+                    fn(x, b, g)
+            if n < n_blocks:
+                for h in range(2):
+                    fill_half(n, h)
+                    evacuate_half(n, h)
+            if 0 <= n - LAG_TR < n_blocks:
+                transpose_e(n - LAG_TR)
+            for x, b, w, h in tensor_extras.get(n, []):
+                transpose_x(x, b, w, h, "t", engine="s")
+            if 0 <= n - LAG_EXP < n_blocks:
+                exponentials(n - LAG_EXP)
+            if 0 <= n - LAG_TR < n_blocks:
+                regroup_e(n - LAG_TR)
+            if 0 <= n - LAG_MX < n_blocks:
+                product(n - LAG_MX)
+                finish(n - LAG_MX)

@@ -18,14 +18,16 @@ TILES = L // P
 SCALE = 1.0 / math.sqrt(D)
 FLOPS = 3 * 2 * B * L * L * D
 
-LAG_EXP = 1
-LAG_TR = 2
-LAG_Q = 3
-LAG_MX = 4
+OPT = {
+    "weave": 0, "lag_exp": 1, "lag_tr": 2, "lag_c": 2, "lag_q": 3, "lag_mx": 4, "pair_mx": False, "f1_v_from": 8,
+    "ebufs": 4, "gbufs": 3, "stbufs": 3, "c_on_v": (), "q_first": True, "units_start": 0, "extras_eng": "s",
+    "manual": True, "obufs": 2, "tbufs": 2, "rbufs": 4, "otbufs": 3, "extras_start": 1,
+}
 
 
 def tile_mutualcrossattention_kernel(tc, x1, x2, out):
     nc = tc.nc
+    O = OPT
     dram = {"x1": x1, "x2": x2}
     with ExitStack() as ctx:
         const = ctx.enter_context(tc.tile_pool(name="const", bufs=1))
@@ -34,13 +36,15 @@ def tile_mutualcrossattention_kernel(tc, x1, x2, out):
         xqp = ctx.enter_context(tc.tile_pool(name="xqp", bufs=1))
         xgp = ctx.enter_context(tc.tile_pool(name="xgp", bufs=2))
         ssb = ctx.enter_context(tc.tile_pool(name="ssb", bufs=1))
-        stp = ctx.enter_context(tc.tile_pool(name="stp", bufs=3))
-        ep = ctx.enter_context(tc.tile_pool(name="ep", bufs=4))
-        gp = ctx.enter_context(tc.tile_pool(name="gp", bufs=3))
+        stp = ctx.enter_context(tc.tile_pool(name="stp", bufs=O["stbufs"]))
+        ep = ctx.enter_context(tc.tile_pool(name="ep", bufs=O["ebufs"]))
+        gp = ctx.enter_context(tc.tile_pool(name="gp", bufs=O["gbufs"]))
         tmpp = ctx.enter_context(tc.tile_pool(name="tmpp", bufs=10))
-        otp = ctx.enter_context(tc.tile_pool(name="otp", bufs=3))
-        small = ctx.enter_context(tc.tile_pool(name="small", bufs=8))
+        otp = ctx.enter_context(tc.tile_pool(name="otp", bufs=O["otbufs"]))
+        small = ctx.enter_context(tc.tile_pool(name="small", bufs=10))
         psum = ctx.enter_context(tc.psum_pool(name="psum", bufs=2))
+        if O["manual"]:
+            ctx.enter_context(tc.manual_schedule())
 
         ident_f = const.tile([P, P], F32, name="ident_f", tag="ident_f")
         ident_b = const.tile([P, P], BF16, name="ident_b", tag="ident_b")
@@ -59,20 +63,19 @@ def tile_mutualcrossattention_kernel(tc, x1, x2, out):
             dst = raw[x, b][:].rearrange("q (c e) d -> q c (e d)", e=2)
             nc.sync.dma_start(out=dst[:, c, :], in_=src[:, c, :])
 
+        make_identity(nc, ident_f[:])
+        make_identity(nc, ident_b[:])
         for b in range(B):
             for half in range(2):
                 for x in ("x2", "x1"):
                     for c in (2 * half, 2 * half + 1):
                         load(x, b, c)
 
-        make_identity(nc, ident_f[:])
-        make_identity(nc, ident_b[:])
-
         copy_turn = [0]
 
-        def transpose_x(x, b, w, h, tag, engine=None):
+        def transpose_x(x, b, w, h, tag, engine=None, later=False):
             words = raw[x, b][:].bitcast(F32)
-            bank = psum.tile([P, 4, P], F32, name="xbank", tag=tag, bufs=(4 if tag == "r" else 2))
+            bank = psum.tile([P, 4, P], F32, name="xbank", tag=tag, bufs=(O["rbufs"] if tag == "r" else O["tbufs"]))
             for k in range(4):
                 nc.tensor.transpose(bank[:, k, :], words[:, 4 * h + k, P * w:P * (w + 1)], ident_f[:])
             dst = xt[x, b][:].bitcast(F32)[:, w, 512 * h:512 * (h + 1)]
@@ -80,10 +83,16 @@ def tile_mutualcrossattention_kernel(tc, x1, x2, out):
             if engine is None:
                 engine = ("v", "s")[copy_turn[0] % 2]
                 copy_turn[0] += 1
-            if engine == "v":
-                nc.vector.tensor_copy(out=dst, in_=src)
-            else:
-                nc.scalar.copy(out=dst, in_=src)
+            def copy_out():
+                if engine == "v":
+                    nc.vector.tensor_copy(out=dst, in_=src)
+                else:
+                    nc.scalar.copy(out=dst, in_=src)
+
+            if later:
+                return copy_out
+            copy_out()
+            return None
 
         grouped = {}
 
@@ -112,26 +121,31 @@ def tile_mutualcrossattention_kernel(tc, x1, x2, out):
         st = [dict() for blk in blocks]
         tmp = {}
 
-        def fill_half(n, h):
+        def fill_items(n, h):
             kind, b, k = blocks[n]
-            bank = psum.tile([P, 4, P], F32, name="rbank", tag="r", bufs=4)
-            st[n]["bank%d" % h] = bank
-            if kind == "s":
-                a = xt["x1", b][:].rearrange("p w (n e) -> p w n e", e=2)
-                m = xt["x2", b][:].rearrange("p w (n e) -> p w n e", e=2)
-                flat = bank[:].rearrange("p k q -> p (k q)")
-                for c in range(4):
+            items = []
+
+            def one(c):
+                if c == 0:
+                    st[n]["bank%d" % h] = psum.tile([P, 4, P], F32, name="rbank", tag="r", bufs=O["rbufs"])
+                bank = st[n]["bank%d" % h]
+                if kind == "s":
+                    a = xt["x1", b][:].rearrange("p w (n e) -> p w n e", e=2)
+                    m = xt["x2", b][:].rearrange("p w (n e) -> p w n e", e=2)
                     w, e = c // 2, c % 2
                     nc.tensor.matmul(
-                        out=flat,
+                        out=bank[:].rearrange("p k q -> p (k q)"),
                         lhsT=a[:, w, P * k:P * (k + 1), e],
                         rhs=m[:, w, 512 * h:512 * (h + 1), e],
                         start=(c == 0),
                         stop=(c == 3),
                     )
-            else:
-                for j in range(4):
-                    nc.tensor.transpose(bank[:, j, :], saved[b, 4 * h + j][:, P * k:P * (k + 1)], ident_f[:])
+                else:
+                    nc.tensor.transpose(bank[:, c, :], saved[b, 4 * h + c][:, P * k:P * (k + 1)], ident_f[:])
+
+            for c in range(4):
+                items.append((one, c))
+            return items
 
         def evacuate_half(n, h):
             kind, b, k = blocks[n]
@@ -163,16 +177,22 @@ def tile_mutualcrossattention_kernel(tc, x1, x2, out):
                 accum_out=st[n]["sum"][:, 0:1],
             )
 
-        def transpose_e(n):
-            et = psum.tile([P, TILES, P], BF16, name="et", tag="t", bufs=2)
-            st[n]["et"] = et
-            for c in range(TILES):
-                nc.tensor.transpose(et[:, c, :], st[n]["e"][:, P * c:P * (c + 1)], ident_b[:])
+        def transpose_items(n):
+            def one(c):
+                if c == 0:
+                    st[n]["et"] = psum.tile([P, TILES, P], BF16, name="et", tag="t", bufs=O["tbufs"])
+                nc.tensor.transpose(st[n]["et"][:, c, :], st[n]["e"][:, P * c:P * (c + 1)], ident_b[:])
+
+            return [(one, c) for c in range(TILES)]
 
         def regroup_e(n):
             g = gp.tile([P, 2, P, 4], BF16, name="g", tag="g", align_bytes=64)
             st[n]["g"] = g
-            nc.scalar.copy(out=g[:], in_=st[n]["et"][:].rearrange("p (g t) r -> p g r t", g=2))
+            src = st[n]["et"][:].rearrange("p (g t) r -> p g r t", g=2)
+            if n in O["c_on_v"]:
+                nc.vector.tensor_copy(out=g[:], in_=src)
+            else:
+                nc.scalar.copy(out=g[:], in_=src)
 
         def quantise_e(n):
             st[n]["codes"] = gp.tile([P, 2 * P], U32, name="codes", tag="codes", align_bytes=64)
@@ -188,7 +208,7 @@ def tile_mutualcrossattention_kernel(tc, x1, x2, out):
         def product(n):
             kind, b, k = blocks[n]
             x = "x2" if kind == "s" else "x1"
-            acc = psum.tile([P, D], F32, name="acc", tag="o", bufs=2)
+            acc = psum.tile([P, D], F32, name="acc", tag="o", bufs=O["obufs"])
             st[n]["acc"] = acc
             for g in range(2):
                 nc.tensor.matmul_mx(
@@ -206,7 +226,7 @@ def tile_mutualcrossattention_kernel(tc, x1, x2, out):
             if kind == "s":
                 t = tmpp.tile([P, D], F32, name="tmp", tag="tmp")
                 tmp[b, k] = t
-                if n < TILES:
+                if n < O["f1_v_from"]:
                     nc.scalar.activation(out=t[:], in_=st[n]["acc"][:], func=ACT.Copy, scale=st[n]["rec"][:, 0:1])
                 else:
                     nc.vector.tensor_scalar(
@@ -221,38 +241,73 @@ def tile_mutualcrossattention_kernel(tc, x1, x2, out):
                 dst = out[b].rearrange("(c q e) d -> c e q d", c=4, q=P, e=2)
                 nc.sync.dma_start(out=dst[k // 2, k % 2], in_=o[:])
 
-        for x, w, h in (("x2", 0, 0), ("x2", 1, 0), ("x1", 0, 0), ("x1", 1, 0), ("x2", 0, 1), ("x2", 1, 1)):
+        def weave(mains, fills, group):
+            if not mains or group == 0:
+                for fn, c in mains + fills:
+                    fn(c)
+                return
+            n_groups = (len(mains) + group - 1) // group
+            share = (len(fills) + n_groups - 1) // n_groups
+            pos = 0
+            for i in range(n_groups):
+                for fn, c in mains[group * i:group * (i + 1)]:
+                    fn(c)
+                for fn, c in fills[pos:pos + share]:
+                    fn(c)
+                pos += share
+
+        for x, w, h in (("x2", 0, 0), ("x2", 1, 0), ("x1", 0, 0), ("x1", 1, 0), ("x2", 0, 1), ("x2", 1, 1),
+                        ("x1", 0, 1), ("x1", 1, 1)):
             transpose_x(x, 0, w, h, "r")
 
-        tensor_extras = {
-            1: [("x1", 0, 0, 1), ("x1", 0, 1, 1)],
-            2: [("x2", 1, 0, 0), ("x2", 1, 1, 0)],
-            3: [("x2", 1, 0, 1), ("x2", 1, 1, 1)],
-            4: [("x1", 1, 0, 0), ("x1", 1, 1, 0)],
-            5: [("x1", 1, 0, 1), ("x1", 1, 1, 1)],
-        }
+        tensor_extras = {}
+        for i, (x, w, h) in enumerate((("x2", 0, 0), ("x2", 1, 0), ("x2", 0, 1), ("x2", 1, 1), ("x1", 0, 0), ("x1", 1, 0),
+                                       ("x1", 0, 1), ("x1", 1, 1))):
+            tensor_extras[i + O["extras_start"]] = [(x, 1, w, h)]
         units = []
         for x, b in (("x2", 0), ("x1", 0), ("x2", 1), ("x1", 1)):
             units += [[(regroup_x, x, b, 0)], [(regroup_x, x, b, 1)], [(quantise_x, x, b, 0), (quantise_x, x, b, 1)]]
 
-        for n in range(n_blocks + LAG_MX + 1):
-            if 0 <= n - LAG_Q < n_blocks:
-                quantise_e(n - LAG_Q)
-            if n < len(units):
-                for fn, x, b, g in units[n]:
+        def ok(m):
+            return 0 <= m < n_blocks
+
+        for n in range(n_blocks + O["lag_mx"] + 2):
+            if O["q_first"] and ok(n - O["lag_q"]):
+                quantise_e(n - O["lag_q"])
+            u = n - O["units_start"]
+            if 0 <= u < len(units):
+                for fn, x, b, g in units[u]:
                     fn(x, b, g)
+            fills = transpose_items(n - O["lag_tr"]) if ok(n - O["lag_tr"]) else []
             if n < n_blocks:
-                for h in range(2):
-                    fill_half(n, h)
-                    evacuate_half(n, h)
-            if 0 <= n - LAG_TR < n_blocks:
-                transpose_e(n - LAG_TR)
-            for x, b, w, h in tensor_extras.get(n, []):
-                transpose_x(x, b, w, h, "t", engine="s")
-            if 0 <= n - LAG_EXP < n_blocks:
-                exponentials(n - LAG_EXP)
-            if 0 <= n - LAG_TR < n_blocks:
-                regroup_e(n - LAG_TR)
-            if 0 <= n - LAG_MX < n_blocks:
-                product(n - LAG_MX)
-                finish(n - LAG_MX)
+                mains = fill_items(n, 0) + fill_items(n, 1)
+                if blocks[n][0] == "s":
+                    weave(mains, fills, O["weave"])
+                else:
+                    weave(mains + fills, [], 0)
+                evacuate_half(n, 0)
+                evacuate_half(n, 1)
+            else:
+                weave([], fills, 0)
+            copies = [transpose_x(x, b, w, h, "t", engine=O["extras_eng"], later=True)
+                      for x, b, w, h in tensor_extras.get(n, [])]
+            if not O["q_first"] and ok(n - O["lag_q"]):
+                quantise_e(n - O["lag_q"])
+            if ok(n - O["lag_exp"]):
+                exponentials(n - O["lag_exp"])
+            if ok(n - O["lag_c"]):
+                regroup_e(n - O["lag_c"])
+            for fn in copies:
+                fn()
+            m = n - O["lag_mx"]
+            if O["pair_mx"]:
+                if n % 2 == 0:
+                    for mm in (m - 1, m):
+                        if ok(mm):
+                            product(mm)
+                    for mm in (m - 1, m):
+                        if ok(mm):
+                            finish(mm)
+            elif ok(m):
+                product(m)
+                finish(m)

@@ -19,7 +19,7 @@ SCALE = 1.0 / math.sqrt(D)
 FLOPS = 3 * 2 * B * L * L * D
 
 OPT = {
-    "weave": 0, "lag_exp": 1, "lag_tr": 2, "lag_c": 2, "lag_q": 3, "lag_mx": 4, "pair_mx": False, "f1_v_from": 8,
+    "weave": 4, "lag_exp": 1, "lag_tr": 2, "lag_c": 2, "lag_q": 3, "lag_mx": 4, "pair_mx": False, "f1_v_from": 8,
     "ebufs": 4, "gbufs": 3, "stbufs": 3, "c_on_v": (), "q_first": True, "units_start": 0, "extras_eng": "s",
     "manual": True, "obufs": 2, "tbufs": 2, "rbufs": 4, "otbufs": 3, "extras_start": 1,
 }

@@ -19,7 +19,7 @@ SCALE = 1.0 / math.sqrt(D)
 FLOPS = 3 * 2 * B * L * L * D
 
 OPT = {
-    "weave": 4, "lag_exp": 1, "lag_tr": 2, "lag_c": 2, "lag_q": 3, "lag_mx": 4, "pair_mx": False, "f1_v_from": 8,
+    "weave": 4, "lag_exp": 1, "lag_tr": 2, "lag_c": 2, "lag_q": 3, "lag_mx": 4, "pair_mx": False, "f1_v_from": 0,
     "ebufs": 4, "gbufs": 3, "stbufs": 3, "c_on_v": (), "q_first": True, "units_start": 0, "extras_eng": "s",
     "manual": True, "obufs": 2, "tbufs": 2, "rbufs": 4, "otbufs": 3, "extras_start": 1,
 }

from contextlib import ExitStack
import math

import concourse.mybir as mybir
from concourse.masks import make_identity

F32 = mybir.dt.float32
BF16 = mybir.dt.bfloat16
U32 = mybir.dt.uint32
U8 = mybir.dt.uint8
FP8X4 = mybir.dt.float8_e4m3fn_x4
ALU = mybir.AluOpType
ACT = mybir.ActivationFunctionType

P = 128
B, L, D = 2, 1024, 512
TILES = L // P
SCALE = 1.0 / math.sqrt(D)
FLOPS = 3 * 2 * B * L * L * D

OPT = {
    "weave": 4, "lag_exp": 1, "lag_tr": 2, "lag_c": 2, "lag_q": 3, "lag_mx": 4, "pair_mx": False, "f1_v_from": 0,
    "ebufs": 4, "gbufs": 3, "stbufs": 3, "c_on_v": (), "q_first": True, "units_start": 0, "extras_eng": "s",
    "manual": True, "obufs": 2, "tbufs": 2, "rbufs": 4, "otbufs": 3, "extras_start": 1,
}


def tile_mutualcrossattention_kernel(tc, x1, x2, out):
    nc = tc.nc
    O = OPT
    dram = {"x1": x1, "x2": x2}
    with ExitStack() as ctx:
        const = ctx.enter_context(tc.tile_pool(name="const", bufs=1))
        xin = ctx.enter_context(tc.tile_pool(name="xin", bufs=1))
        xtp = ctx.enter_context(tc.tile_pool(name="xtp", bufs=1))
        xqp = ctx.enter_context(tc.tile_pool(name="xqp", bufs=1))
        xgp = ctx.enter_context(tc.tile_pool(name="xgp", bufs=2))
        ssb = ctx.enter_context(tc.tile_pool(name="ssb", bufs=1))
        stp = ctx.enter_context(tc.tile_pool(name="stp", bufs=O["stbufs"]))
        ep = ctx.enter_context(tc.tile_pool(name="ep", bufs=O["ebufs"]))
        gp = ctx.enter_context(tc.tile_pool(name="gp", bufs=O["gbufs"]))
        tmpp = ctx.enter_context(tc.tile_pool(name="tmpp", bufs=10))
        otp = ctx.enter_context(tc.tile_pool(name="otp", bufs=O["otbufs"]))
        small = ctx.enter_context(tc.tile_pool(name="small", bufs=10))
        psum = ctx.enter_context(tc.psum_pool(name="psum", bufs=2))
        if O["manual"]:
            ctx.enter_context(tc.manual_schedule())

        ident_f = const.tile([P, P], F32, name="ident_f", tag="ident_f")
        ident_b = const.tile([P, P], BF16, name="ident_b", tag="ident_b")

        keys = [(x, b) for b in range(B) for x in ("x2", "x1")]
        raw, xt, xcodes, xscales = {}, {}, {}, {}
        for x, b in keys:
            nm = "%s_%d" % (x, b)
            raw[x, b] = xin.tile([P, TILES, D], BF16, name="raw_" + nm, tag="raw_" + nm)
            xt[x, b] = xtp.tile([P, 2, 2 * L], BF16, name="xt_" + nm, tag="xt_" + nm)
            xcodes[x, b] = xqp.tile([P, 2, D], U32, name="xc_" + nm, tag="xc_" + nm, align_bytes=64)
            xscales[x, b] = xqp.tile([P, 2, D], U8, name="xs_" + nm, tag="xs_" + nm, align_bytes=64)

        def load(x, b, c):
            src = dram[x][b].rearrange("(c q e) d -> q c (e d)", c=4, q=P, e=2)
            dst = raw[x, b][:].rearrange("q (c e) d -> q c (e d)", e=2)
            nc.sync.dma_start(out=dst[:, c, :], in_=src[:, c, :])

        make_identity(nc, ident_f[:])
        make_identity(nc, ident_b[:])
        for b in range(B):
            for half in range(2):
                for x in ("x2", "x1"):
                    for c in (2 * half, 2 * half + 1):
                        load(x, b, c)

        copy_turn = [0]

        def transpose_x(x, b, w, h, tag, engine=None, later=False):
            words = raw[x, b][:].bitcast(F32)
            bank = psum.tile([P, 4, P], F32, name="xbank", tag=tag, bufs=(O["rbufs"] if tag == "r" else O["tbufs"]))
            for k in range(4):
                nc.tensor.transpose(bank[:, k, :], words[:, 4 * h + k, P * w:P * (w + 1)], ident_f[:])
            dst = xt[x, b][:].bitcast(F32)[:, w, 512 * h:512 * (h + 1)]
            src = bank[:].rearrange("p k q -> p (k q)")
            if engine is None:
                engine = ("v", "s")[copy_turn[0] % 2]
                copy_turn[0] += 1
            def copy_out():
                if engine == "v":
                    nc.vector.tensor_copy(out=dst, in_=src)
                else:
                    nc.scalar.copy(out=dst, in_=src)

            if later:
                return copy_out
            copy_out()
            return None

        grouped = {}

        def regroup_x(x, b, g):
            t = xgp.tile([P, D, 4], BF16, name="xg", tag="xg", align_bytes=64)
            grouped[x, b, g] = t
            nc.vector.tensor_copy(
                out=t[:].rearrange("p (c i) t -> p c t i", i=4),
                in_=raw[x, b][:, 4 * g:4 * g + 4, :].rearrange("p t (c i) -> p c t i", i=4),
            )

        def quantise_x(x, b, g):
            nc.vector.quantize_mx(
                out=xcodes[x, b][:, g, :].bitcast(FP8X4),
                scales=xscales[x, b][:, g, :],
                in_=grouped[x, b, g][:].rearrange("p d t -> p (d t)"),
            )

        blocks = [("s", 0, k) for k in range(TILES)]
        for k in range(TILES):
            blocks += [("s", 1, k), ("t", 0, k)]
        blocks += [("t", 1, k) for k in range(TILES)]
        n_blocks = len(blocks)

        saved = {}
        st = [dict() for blk in blocks]
        tmp = {}

        def fill_items(n, h):
            kind, b, k = blocks[n]
            items = []

            def one(c):
                if c == 0:
                    st[n]["bank%d" % h] = psum.tile([P, 4, P], F32, name="rbank", tag="r", bufs=O["rbufs"])
                bank = st[n]["bank%d" % h]
                if kind == "s":
                    a = xt["x1", b][:].rearrange("p w (n e) -> p w n e", e=2)
                    m = xt["x2", b][:].rearrange("p w (n e) -> p w n e", e=2)
                    w, e = c // 2, c % 2
                    nc.tensor.matmul(
                        out=bank[:].rearrange("p k q -> p (k q)"),
                        lhsT=a[:, w, P * k:P * (k + 1), e],
                        rhs=m[:, w, 512 * h:512 * (h + 1), e],
                        start=(c == 0),
                        stop=(c == 3),
                    )
                else:
                    nc.tensor.transpose(bank[:, c, :], saved[b, 4 * h + c][:, P * k:P * (k + 1)], ident_f[:])

            for c in range(4):
                items.append((one, c))
            return items

        def evacuate_half(n, h):
            kind, b, k = blocks[n]
            if h == 0:
                if kind == "s":
                    rows = ssb.tile([P, L], F32, name="s_%d_%d" % (b, k), tag="s_%d_%d" % (b, k))
                    saved[b, k] = rows
                else:
                    rows = stp.tile([P, L], F32, name="st", tag="st")
                st[n]["rows"] = rows
                st[n]["nb0"] = small.tile([P, 1], F32, name="nb0", tag="nb0")
                st[n]["nb"] = small.tile([P, 1], F32, name="nb", tag="nb")
            nc.vector.tensor_scalar(
                out=st[n]["rows"][:, 512 * h:512 * (h + 1)],
                in0=st[n]["bank%d" % h][:].rearrange("p k q -> p (k q)"),
                scalar1=(-SCALE if kind == "s" else 1.0),
                scalar2=(None if h == 0 else st[n]["nb0"][:, 0:1]),
                op0=ALU.mult,
                op1=ALU.min,
                accum_out=(st[n]["nb0"] if h == 0 else st[n]["nb"])[:, 0:1],
            )

        def exponentials(n):
            e = ep.tile([P, L], BF16, name="e", tag="e")
            st[n]["e"] = e
            st[n]["sum"] = small.tile([P, 1], F32, name="sum", tag="sum")
            nc.scalar.activation(
                out=e[:], in_=st[n]["rows"][:], func=ACT.Exp, bias=st[n]["nb"][:, 0:1], scale=-1.0,
                accum_out=st[n]["sum"][:, 0:1],
            )

        def transpose_items(n):
            def one(c):
                if c == 0:
                    st[n]["et"] = psum.tile([P, TILES, P], BF16, name="et", tag="t", bufs=O["tbufs"])
                nc.tensor.transpose(st[n]["et"][:, c, :], st[n]["e"][:, P * c:P * (c + 1)], ident_b[:])

            return [(one, c) for c in range(TILES)]

        def regroup_e(n):
            g = gp.tile([P, 2, P, 4], BF16, name="g", tag="g", align_bytes=64)
            st[n]["g"] = g
            src = st[n]["et"][:].rearrange("p (g t) r -> p g r t", g=2)
            if n in O["c_on_v"]:
                nc.vector.tensor_copy(out=g[:], in_=src)
            else:
                nc.scalar.copy(out=g[:], in_=src)

        def quantise_e(n):
            st[n]["codes"] = gp.tile([P, 2 * P], U32, name="codes", tag="codes", align_bytes=64)
            st[n]["scales"] = gp.tile([P, 2 * P], U8, name="scales", tag="scales", align_bytes=64)
            nc.vector.quantize_mx(
                out=st[n]["codes"][:].bitcast(FP8X4),
                scales=st[n]["scales"][:],
                in_=st[n]["g"][:].rearrange("p g r t -> p (g r t)"),
            )
            st[n]["rec"] = small.tile([P, 1], F32, name="rec", tag="rec")
            nc.vector.reciprocal(out=st[n]["rec"][:, 0:1], in_=st[n]["sum"][:, 0:1])

        def product(n):
            kind, b, k = blocks[n]
            x = "x2" if kind == "s" else "x1"
            acc = psum.tile([P, D], F32, name="acc", tag="o", bufs=O["obufs"])
            st[n]["acc"] = acc
            for g in range(2):
                nc.tensor.matmul_mx(
                    out=acc[:],
                    lhsT=st[n]["codes"][:, P * g:P * (g + 1)].bitcast(FP8X4),
                    lhsT_scale=st[n]["scales"][:, P * g:P * (g + 1)],
                    rhs=xcodes[x, b][:, g, :].bitcast(FP8X4),
                    rhs_scale=xscales[x, b][:, g, :],
                    start=(g == 0),
                    stop=(g == 1),
                )

        def finish(n):
            kind, b, k = blocks[n]
            if kind == "s":
                t = tmpp.tile([P, D], F32, name="tmp", tag="tmp")
                tmp[b, k] = t
                if n < O["f1_v_from"]:
                    nc.scalar.activation(out=t[:], in_=st[n]["acc"][:], func=ACT.Copy, scale=st[n]["rec"][:, 0:1])
                else:
                    nc.vector.tensor_scalar(
                        out=t[:], in0=st[n]["acc"][:], scalar1=st[n]["rec"][:, 0:1], scalar2=None, op0=ALU.mult
                    )
            else:
                o = otp.tile([P, D], F32, name="o", tag="o")
                nc.vector.scalar_tensor_tensor(
                    out=o[:], in0=st[n]["acc"][:], scalar=st[n]["rec"][:, 0:1], in1=tmp[b, k][:],
                    op0=ALU.mult, op1=ALU.add,
                )
                dst = out[b].rearrange("(c q e) d -> c e q d", c=4, q=P, e=2)
                nc.sync.dma_start(out=dst[k // 2, k % 2], in_=o[:])

        def weave(mains, fills, group):
            if not mains or group == 0:
                for fn, c in mains + fills:
                    fn(c)
                return
            n_groups = (len(mains) + group - 1) // group
            share = (len(fills) + n_groups - 1) // n_groups
            pos = 0
            for i in range(n_groups):
                for fn, c in mains[group * i:group * (i + 1)]:
                    fn(c)
                for fn, c in fills[pos:pos + share]:
                    fn(c)
                pos += share

        for x, w, h in (("x2", 0, 0), ("x2", 1, 0), ("x1", 0, 0), ("x1", 1, 0), ("x2", 0, 1), ("x2", 1, 1),
                        ("x1", 0, 1), ("x1", 1, 1)):
            transpose_x(x, 0, w, h, "r")

        tensor_extras = {}
        for i, (x, w, h) in enumerate((("x2", 0, 0), ("x2", 1, 0), ("x2", 0, 1), ("x2", 1, 1), ("x1", 0, 0), ("x1", 1, 0),
                                       ("x1", 0, 1), ("x1", 1, 1))):
            tensor_extras[i + O["extras_start"]] = [(x, 1, w, h)]
        units = []
        for x, b in (("x2", 0), ("x1", 0), ("x2", 1), ("x1", 1)):
            units += [[(regroup_x, x, b, 0)], [(regroup_x, x, b, 1)], [(quantise_x, x, b, 0), (quantise_x, x, b, 1)]]

        def ok(m):
            return 0 <= m < n_blocks

        for n in range(n_blocks + O["lag_mx"] + 2):
            if O["q_first"] and ok(n - O["lag_q"]):
                quantise_e(n - O["lag_q"])
            u = n - O["units_start"]
            if 0 <= u < len(units):
                for fn, x, b, g in units[u]:
                    fn(x, b, g)
            fills = transpose_items(n - O["lag_tr"]) if ok(n - O["lag_tr"]) else []
            if n < n_blocks:
                mains = fill_items(n, 0) + fill_items(n, 1)
                if blocks[n][0] == "s":
                    weave(mains, fills, O["weave"])
                else:
                    weave(mains + fills, [], 0)
                evacuate_half(n, 0)
                evacuate_half(n, 1)
            else:
                weave([], fills, 0)
            copies = [transpose_x(x, b, w, h, "t", engine=O["extras_eng"], later=True)
                      for x, b, w, h in tensor_extras.get(n, [])]
            if not O["q_first"] and ok(n - O["lag_q"]):
                quantise_e(n - O["lag_q"])
            if ok(n - O["lag_exp"]):
                exponentials(n - O["lag_exp"])
            if ok(n - O["lag_c"]):
                regroup_e(n - O["lag_c"])
            for fn in copies:
                fn()
            m = n - O["lag_mx"]
            if O["pair_mx"]:
                if n % 2 == 0:
                    for mm in (m - 1, m):
                        if ok(mm):
                            product(mm)
                    for mm in (m - 1, m):
                        if ok(mm):
                            finish(mm)
            elif ok(m):
                product(m)
                finish(m)
